import numpy as np
import ml_dtypes


def mxq(x, axis, fmt="e4m3"):
    dtype, down = {"e4m3": (ml_dtypes.float8_e4m3fn, 7), "e5m2": (ml_dtypes.float8_e5m2, 14)}[fmt]
    v = np.moveaxis(np.asarray(x, np.float32).astype(ml_dtypes.bfloat16).astype(np.float64), axis, -1)
    blocks = v.reshape(v.shape[:-1] + (-1, 32))
    amax = np.abs(blocks).max(-1, keepdims=True)
    byte = np.maximum(np.where(amax > 0, np.frexp(amax)[1] - 1 + 127, 0) - down, 1)
    scale = np.exp2(byte - 127.0)
    codes = (blocks / scale).astype(np.float32).astype(dtype).astype(np.float64)
    return np.moveaxis((codes * scale).reshape(v.shape), -1, axis)


WIDE = False


def mx_kscale(k):
    if not WIDE:
        return np.ones(k)
    levels = np.array([10, -10, 5, -5, 0])
    a = np.random.permutation(np.resize(levels, k // 512 * 4)).reshape(k // 512, 4)
    idx = np.arange(k)
    return np.exp2(a[idx // 512, idx % 128 // 32])


BF16 = ml_dtypes.bfloat16


def bf(x):
    return np.asarray(x, np.float32).astype(BF16)


def f64(x):
    return np.asarray(x).astype(np.float64)


B, L, H, U = 2, 4096, 512, 512
R_MIN, R_MAX = 0.9, 0.999


def setup_inputs():
    s, t = mx_kscale(H), mx_kscale(U)
    inputs = np.random.standard_normal((B, L, H)) * s
    Wi = np.random.standard_normal((U, H)) / np.sqrt(H) / s[None, :] * t[:, None]
    bi = np.random.standard_normal(U) * 0.03 * t
    Wo = np.random.standard_normal((H, U)) / np.sqrt(U) / t[None, :]
    bo = np.random.standard_normal(H) * 0.1
    r = np.random.uniform(size=U)
    nu_log = np.log(-0.5 * np.log(r * (R_MAX ** 2 - R_MIN ** 2) + R_MIN ** 2))
    gamma_log = np.log(np.sqrt(1.0 - np.exp(-np.exp(nu_log)) ** 2))
    params_log = np.stack([nu_log, gamma_log])
    return {"inputs": bf(inputs), "Wi": bf(Wi), "bi": bf(bi), "Wo": bf(Wo), "bo": bf(bo), "params_log": bf(params_log)}


def reference(inputs, Wi, bi, Wo, bo, params_log):
    u = (mxq(f64(inputs), 2, "e4m3") @ mxq(f64(Wi), 1, "e4m3").T) + f64(bi)
    params = np.exp(f64(params_log))
    nu, gamma = params[0], params[1]

    log2_L = int(np.ceil(np.log2(L)))
    pad_len = 2 ** log2_L - L
    x = np.pad(u, ((0, 0), (0, pad_len), (0, 0))) if pad_len else u
    Lp = 2 ** log2_L

    for i in range(1, log2_L + 1):
        l = 2 ** i
        x = x.reshape(B * Lp // l, l, U)
        x1, x2 = x[:, : l // 2], x[:, l // 2:]
        pos = np.arange(1, l // 2 + 1, dtype=np.float64)
        lambs = np.exp(-pos[:, None] * nu)
        x2 = x2 + lambs * x1[:, -1:]
        x = np.concatenate([x1, x2], axis=1).reshape(B, Lp, U)

    x = x[:, :L] * gamma
    return (mxq(x, 2, "e4m3") @ mxq(f64(Wo), 1, "e4m3").T) + f64(bo)

@@ -1,0 +1,175 @@
+from contextlib import ExitStack
+
+import concourse.mybir as mybir
+from concourse.masks import make_identity
+
+F32 = mybir.dt.float32
+BF16 = mybir.dt.bfloat16
+U32 = mybir.dt.uint32
+U8 = mybir.dt.uint8
+FP8X4 = mybir.dt.float8_e4m3fn_x4
+ACT = mybir.ActivationFunctionType
+ALU = mybir.AluOpType
+
+P = 128
+BATCH = 2
+SEQ = 4096
+FEAT = 512
+CHAN = 512
+TOKENS = BATCH * SEQ
+BLOCK = 512
+SUB = BLOCK // P
+ROUNDS = TOKENS // BLOCK
+ROUNDS_PER_SEQ = SEQ // BLOCK
+FLOPS = 2 * TOKENS * FEAT * CHAN * 2
+
+
+def tile_slru_t_kernel(tc, inputs, Wi, bi, Wo, bo, params_log, out):
+    nc = tc.nc
+    x_flat = inputs.flatten_outer_dims()
+    out_flat = out.flatten_outer_dims()
+
+    with ExitStack() as ctx:
+        const = ctx.enter_context(tc.tile_pool(name="const", bufs=1))
+        rows = ctx.enter_context(tc.tile_pool(name="rows", bufs=3))
+        grp = ctx.enter_context(tc.tile_pool(name="grp", bufs=2))
+        mxin = ctx.enter_context(tc.tile_pool(name="mxin", bufs=2))
+        upool = ctx.enter_context(tc.tile_pool(name="upool", bufs=4))
+        xpool = ctx.enter_context(tc.tile_pool(name="xpool", bufs=3))
+        opool = ctx.enter_context(tc.tile_pool(name="opool", bufs=3))
+        ps_t = ctx.enter_context(tc.psum_pool(name="ps_t", bufs=2))
+        ps_u = ctx.enter_context(tc.psum_pool(name="ps_u", bufs=3))
+        ps_o = ctx.enter_context(tc.psum_pool(name="ps_o", bufs=3))
+
+        ident = const.tile([P, P], F32)
+        make_identity(nc, ident[:])
+
+        def transpose_and_quantise(src, codes, scales):
+            src32 = src[:].bitcast(F32)
+            grouped = grp.tile([P, 4 * BLOCK], BF16, align_bytes=64)
+            g32 = grouped[:].bitcast(F32).rearrange("p (c u) -> p c u", u=2)
+            for half in range(2):
+                bank = ps_t.tile([P, 2, 2, P], F32, tag="bank_t")
+                for s in range(2):
+                    for u in range(2):
+                        first = (2 * half + s) * 256 + u * P
+                        nc.tensor.transpose(bank[:, s, u, :], src32[:, first : first + P], ident[:])
+                nc.scalar.copy(
+                    out=g32[:, half * 256 : (half + 1) * 256, :].rearrange("p (s r) u -> p s r u", s=2),
+                    in_=bank[:].rearrange("p s u r -> p s r u"),
+                )
+            nc.vector.quantize_mx(out=codes[:].bitcast(FP8X4), scales=scales[:], in_=grouped[:])
+
+        prow = const.tile([P, 2 * P], BF16)
+        nc.vector.memset(prow[:], 0.0)
+        nc.scalar.dma_start(out=prow[0:4, :], in_=params_log.rearrange("v (u w) -> (v u) w", u=2))
+        nc.scalar.dma_start(out=prow[4:6, :], in_=bi.rearrange("(u w) -> u w", u=2))
+
+        wi_sb = const.tile([P, 4 * FEAT], BF16)
+        nc.sync.dma_start(
+            out=wi_sb[:].rearrange("p (u e h) -> p u e h", u=2, e=2),
+            in_=Wi.rearrange("(u p e) h -> p u e h", u=2, e=2),
+        )
+
+        def load_round(i):
+            x_sb = rows.tile([P, SUB * FEAT], BF16, tag="x_sb")
+            nc.sync.dma_start(
+                out=x_sb[:].rearrange("p (s h) -> p s h", s=SUB),
+                in_=x_flat[i * BLOCK : (i + 1) * BLOCK, :].rearrange("(s p) h -> p s h", p=P),
+            )
+            return x_sb
+
+        x_first = load_round(0)
+
+        wo_sb = const.tile([P, 4 * CHAN], BF16)
+        nc.sync.dma_start(
+            out=wo_sb[:].rearrange("p (a c) -> p a c", a=4),
+            in_=Wo.rearrange("(a p) c -> p a c", p=P),
+        )
+        bo_bf = const.tile([P, FEAT], BF16)
+        nc.scalar.dma_start(out=bo_bf[:], in_=bo.partition_broadcast(P))
+
+        pbank = ps_t.tile([P, 2, 2, P], F32, tag="bank_t")
+        nc.tensor.transpose(pbank[:, 0, 0, :], prow[:].bitcast(F32), ident[:])
+        pwords = const.tile([P, 8], F32)
+        nc.vector.tensor_copy(out=pwords[:], in_=pbank[:, 0, 0, 0:8])
+        pcol = pwords[:].bitcast(BF16)
+        nu = const.tile([P, 4], F32)
+        nc.scalar.activation(out=nu[:], in_=pcol[:, 0:4], func=ACT.Exp)
+        lam = const.tile([P, 4], F32)
+        nc.scalar.activation(out=lam[:], in_=nu[:], func=ACT.Exp, scale=-1.0)
+        gam = const.tile([P, 4], F32)
+        nc.scalar.activation(out=gam[:], in_=pcol[:, 4:8], func=ACT.Exp)
+        gbi = const.tile([P, 4], F32)
+        nc.vector.tensor_tensor(out=gbi[:], in0=gam[:], in1=pcol[:, 8:12], op=ALU.mult)
+
+        wi_codes = const.tile([P, CHAN], U32, align_bytes=64)
+        wi_scales = const.tile([P, CHAN], U8, align_bytes=64)
+        transpose_and_quantise(wi_sb, wi_codes, wi_scales)
+        wo_codes = const.tile([P, FEAT], U32, align_bytes=64)
+        wo_scales = const.tile([P, FEAT], U8, align_bytes=64)
+
+        bo32 = const.tile([P, FEAT], F32)
+
+        previous = None
+        for i in range(ROUNDS):
+            x_sb = x_first if i == 0 else load_round(i)
+            in_codes = mxin.tile([P, BLOCK], U32, align_bytes=64, tag="in_codes")
+            in_scales = mxin.tile([P, BLOCK], U8, align_bytes=64, tag="in_scales")
+            transpose_and_quantise(x_sb, in_codes, in_scales)
+
+            xs = xpool.tile([P, 4, BLOCK], F32, tag="xs")
+            for j in range(4):
+                u_ps = ps_u.tile([P, BLOCK], F32, tag="u_ps")
+                nc.tensor.matmul_mx(
+                    out=u_ps[:],
+                    lhsT=wi_codes[:, j * P : (j + 1) * P].bitcast(FP8X4),
+                    lhsT_scale=wi_scales[:, j * P : (j + 1) * P],
+                    rhs=in_codes[:].bitcast(FP8X4),
+                    rhs_scale=in_scales[:],
+                    start=True,
+                    stop=True,
+                )
+                u_sb = upool.tile([P, BLOCK], F32, tag="u_sb")
+                nc.scalar.activation(
+                    out=u_sb[:], in_=u_ps[:], func=ACT.Identity, bias=gbi[:, j : j + 1], scale=gam[:, j : j + 1]
+                )
+                start_value = 0.0 if i % ROUNDS_PER_SEQ == 0 else previous[:, j, BLOCK - 1 : BLOCK]
+                nc.vector.tensor_tensor_scan(
+                    out=xs[:, j, :],
+                    data0=lam[:, j : j + 1].to_broadcast([P, BLOCK]),
+                    data1=u_sb[:],
+                    initial=start_value,
+                    op0=ALU.mult,
+                    op1=ALU.add,
+                )
+            previous = xs
+
+            if i == 0:
+                transpose_and_quantise(wo_sb, wo_codes, wo_scales)
+                nc.vector.tensor_copy(out=bo32[:], in_=bo_bf[:])
+
+            xg = grp.tile([P, BLOCK, 4], BF16, align_bytes=64, tag="xg")
+            nc.scalar.copy(out=xg[:], in_=xs[:].rearrange("p j t -> p t j"))
+            x_codes = mxin.tile([P, BLOCK], U32, align_bytes=64, tag="x_codes")
+            x_scales = mxin.tile([P, BLOCK], U8, align_bytes=64, tag="x_scales")
+            nc.vector.quantize_mx(
+                out=x_codes[:].bitcast(FP8X4), scales=x_scales[:], in_=xg[:].rearrange("p t j -> p (t j)")
+            )
+
+            o_sb = opool.tile([P, SUB, FEAT], F32, tag="o_sb")
+            for s in range(SUB):
+                o_ps = ps_o.tile([P, FEAT], F32, tag="o_ps")
+                nc.tensor.matmul_mx(
+                    out=o_ps[:],
+                    lhsT=x_codes[:, s * P : (s + 1) * P].bitcast(FP8X4),
+                    lhsT_scale=x_scales[:, s * P : (s + 1) * P],
+                    rhs=wo_codes[:].bitcast(FP8X4),
+                    rhs_scale=wo_scales[:],
+                    start=True,
+                    stop=True,
+                )
+                nc.vector.tensor_tensor(out=o_sb[:, s, :], in0=o_ps[:], in1=bo32[:], op=ALU.add)
+            nc.sync.dma_start(
+                out=out_flat[i * BLOCK : (i + 1) * BLOCK, :].rearrange("(s p) f -> p s f", p=P), in_=o_sb[:]
+            )

@@ -12,15 +12,14 @@ ACT = mybir.ActivationFunctionType
 ALU = mybir.AluOpType
 
 P = 128
-BATCH = 2
-SEQ = 4096
 FEAT = 512
 CHAN = 512
-TOKENS = BATCH * SEQ
+TOKENS = 8192
 BLOCK = 512
-SUB = BLOCK // P
-ROUNDS = TOKENS // BLOCK
-ROUNDS_PER_SEQ = SEQ // BLOCK
+NBLOCKS = TOKENS // BLOCK
+BLOCKS_PER_SEQ = 8
+SPANS = ((0,), (1,), (2, 3), (4, 5), (6, 7), (8, 9), (10, 11), (12, 13), (14,), (15,))
+G_TILES = (1, 1, 1, 2, 1, 2, 1, 2, 1, 2, 1, 2, 1, 2, 1, 0)
 FLOPS = 2 * TOKENS * FEAT * CHAN * 2
 
 
@@ -28,66 +27,105 @@ def tile_slru_t_kernel(tc, inputs, Wi, bi, Wo, bo, params_log, out):
     nc = tc.nc
     x_flat = inputs.flatten_outer_dims()
     out_flat = out.flatten_outer_dims()
+    n_spans = len(SPANS)
+    where = {}
+    for si in range(n_spans):
+        for k in range(len(SPANS[si])):
+            where[SPANS[si][k]] = (si, k * BLOCK)
+
+    def span(i):
+        return SPANS[i] if 0 <= i < n_spans else ()
 
     with ExitStack() as ctx:
         const = ctx.enter_context(tc.tile_pool(name="const", bufs=1))
-        rows = ctx.enter_context(tc.tile_pool(name="rows", bufs=3))
+        rows = ctx.enter_context(tc.tile_pool(name="rows", bufs=NBLOCKS + 2))
         grp = ctx.enter_context(tc.tile_pool(name="grp", bufs=2))
-        mxin = ctx.enter_context(tc.tile_pool(name="mxin", bufs=2))
-        upool = ctx.enter_context(tc.tile_pool(name="upool", bufs=4))
+        xgp = ctx.enter_context(tc.tile_pool(name="xgp", bufs=3))
+        mxin = ctx.enter_context(tc.tile_pool(name="mxin", bufs=3))
+        upool = ctx.enter_context(tc.tile_pool(name="upool", bufs=2))
         xpool = ctx.enter_context(tc.tile_pool(name="xpool", bufs=3))
-        opool = ctx.enter_context(tc.tile_pool(name="opool", bufs=3))
+        opool = ctx.enter_context(tc.tile_pool(name="opool", bufs=4))
+        ps_l = ctx.enter_context(tc.psum_pool(name="ps_l", bufs=1))
         ps_t = ctx.enter_context(tc.psum_pool(name="ps_t", bufs=2))
-        ps_u = ctx.enter_context(tc.psum_pool(name="ps_u", bufs=3))
+        ps_u = ctx.enter_context(tc.psum_pool(name="ps_u", bufs=2))
         ps_o = ctx.enter_context(tc.psum_pool(name="ps_o", bufs=3))
+        ctx.enter_context(tc.manual_schedule())
 
         ident = const.tile([P, P], F32)
         make_identity(nc, ident[:])
-
-        def transpose_and_quantise(src, codes, scales):
-            src32 = src[:].bitcast(F32)
-            grouped = grp.tile([P, 4 * BLOCK], BF16, align_bytes=64)
-            g32 = grouped[:].bitcast(F32).rearrange("p (c u) -> p c u", u=2)
-            for half in range(2):
-                bank = ps_t.tile([P, 2, 2, P], F32, tag="bank_t")
-                for s in range(2):
-                    for u in range(2):
-                        first = (2 * half + s) * 256 + u * P
-                        nc.tensor.transpose(bank[:, s, u, :], src32[:, first : first + P], ident[:])
-                nc.scalar.copy(
-                    out=g32[:, half * 256 : (half + 1) * 256, :].rearrange("p (s r) u -> p s r u", s=2),
-                    in_=bank[:].rearrange("p s u r -> p s r u"),
-                )
-            nc.vector.quantize_mx(out=codes[:].bitcast(FP8X4), scales=scales[:], in_=grouped[:])
-
         prow = const.tile([P, 2 * P], BF16)
         nc.vector.memset(prow[:], 0.0)
+        lam_pad = const.tile([P, P], F32)
+        nc.vector.memset(lam_pad[:], 0.0)
+        bo_row = const.tile([P, FEAT], BF16)
+        nc.vector.memset(bo_row[:], 0.0)
+        ones = const.tile([P, P], BF16)
+        nc.vector.memset(ones[:], 1.0)
         nc.scalar.dma_start(out=prow[0:4, :], in_=params_log.rearrange("v (u w) -> (v u) w", u=2))
         nc.scalar.dma_start(out=prow[4:6, :], in_=bi.rearrange("(u w) -> u w", u=2))
+        nc.scalar.dma_start(out=bo_row[0:1, :], in_=bo.rearrange("(o f) -> o f", o=1))
 
-        wi_sb = const.tile([P, 4 * FEAT], BF16)
+        wi_sb = rows.tile([P, 4 * FEAT], BF16, tag="rows")
         nc.sync.dma_start(
             out=wi_sb[:].rearrange("p (u e h) -> p u e h", u=2, e=2),
             in_=Wi.rearrange("(u p e) h -> p u e h", u=2, e=2),
         )
+        x_sb = {}
 
-        def load_round(i):
-            x_sb = rows.tile([P, SUB * FEAT], BF16, tag="x_sb")
+        def load(b):
+            x_tile = rows.tile([P, 4 * FEAT], BF16, tag="rows")
             nc.sync.dma_start(
-                out=x_sb[:].rearrange("p (s h) -> p s h", s=SUB),
-                in_=x_flat[i * BLOCK : (i + 1) * BLOCK, :].rearrange("(s p) h -> p s h", p=P),
+                out=x_tile[:].rearrange("p (s h) -> p s h", s=4),
+                in_=x_flat[b * BLOCK : (b + 1) * BLOCK, :].rearrange("(s p) h -> p s h", p=P),
             )
-            return x_sb
+            x_sb[b] = x_tile
 
-        x_first = load_round(0)
-
-        wo_sb = const.tile([P, 4 * CHAN], BF16)
+        for b in range(3):
+            load(b)
+        wo_sb = rows.tile([P, 4 * CHAN], BF16, tag="rows")
         nc.sync.dma_start(
             out=wo_sb[:].rearrange("p (a c) -> p a c", a=4),
             in_=Wo.rearrange("(a p) c -> p a c", p=P),
         )
-        bo_bf = const.tile([P, FEAT], BF16)
-        nc.scalar.dma_start(out=bo_bf[:], in_=bo.partition_broadcast(P))
+        for b in range(3, NBLOCKS):
+            load(b)
+
+        warm = const.tile([P, 1], F32)
+        nc.scalar.activation(out=warm[:], in_=lam_pad[:, 0:1], func=ACT.Exp)
+
+        def transpose_half(src, half):
+            bank = ps_t.tile([P, 2, 2, P], F32, tag="bank_t")
+            src32 = src[:].bitcast(F32)
+            for s2 in range(2):
+                for u in range(2):
+                    first = (2 * half + s2) * 256 + u * P
+                    nc.tensor.transpose(bank[:, s2, u, :], src32[:, first : first + P], ident[:])
+            return bank
+
+        def copy_half(on_scalar, grouped, half, bank):
+            g32 = grouped[:].bitcast(F32).rearrange("p (c u) -> p c u", u=2)
+            dst = g32[:, half * 256 : (half + 1) * 256, :].rearrange("p (s r) u -> p s r u", s=2)
+            view = bank[:].rearrange("p s u r -> p s r u")
+            if on_scalar:
+                nc.scalar.copy(out=dst, in_=view)
+            else:
+                nc.vector.tensor_copy(out=dst, in_=view)
+
+        def quantise(src, codes, scales):
+            nc.vector.quantize_mx(out=codes[:].bitcast(FP8X4), scales=scales[:], in_=src)
+
+        grouped = {}
+        in_mx = {}
+
+        def new_grouped(b):
+            g_tile = grp.tile([P, 4 * BLOCK], BF16, align_bytes=64, tag="grouped")
+            grouped[b] = g_tile
+
+        def q1(b):
+            in_codes = mxin.tile([P, BLOCK], U32, align_bytes=64, tag="in_codes")
+            in_scales = mxin.tile([P, BLOCK], U8, align_bytes=64, tag="in_scales")
+            quantise(grouped[b][:], in_codes, in_scales)
+            in_mx[b] = (in_codes, in_scales)
 
         pbank = ps_t.tile([P, 2, 2, P], F32, tag="bank_t")
         nc.tensor.transpose(pbank[:, 0, 0, :], prow[:].bitcast(F32), ident[:])
@@ -96,80 +134,197 @@ def tile_slru_t_kernel(tc, inputs, Wi, bi, Wo, bo, params_log, out):
         pcol = pwords[:].bitcast(BF16)
         nu = const.tile([P, 4], F32)
         nc.scalar.activation(out=nu[:], in_=pcol[:, 0:4], func=ACT.Exp)
-        lam = const.tile([P, 4], F32)
-        nc.scalar.activation(out=lam[:], in_=nu[:], func=ACT.Exp, scale=-1.0)
+        nc.scalar.activation(out=lam_pad[:, 0:4], in_=nu[:], func=ACT.Exp, scale=-1.0)
         gam = const.tile([P, 4], F32)
         nc.scalar.activation(out=gam[:], in_=pcol[:, 4:8], func=ACT.Exp)
-        gbi = const.tile([P, 4], F32)
-        nc.vector.tensor_tensor(out=gbi[:], in0=gam[:], in1=pcol[:, 8:12], op=ALU.mult)
 
         wi_codes = const.tile([P, CHAN], U32, align_bytes=64)
         wi_scales = const.tile([P, CHAN], U8, align_bytes=64)
-        transpose_and_quantise(wi_sb, wi_codes, wi_scales)
         wo_codes = const.tile([P, FEAT], U32, align_bytes=64)
         wo_scales = const.tile([P, FEAT], U8, align_bytes=64)
 
+        wi_g = grp.tile([P, 4 * BLOCK], BF16, align_bytes=64, tag="grouped")
+        bank0 = transpose_half(wi_sb, 0)
+        bank1 = transpose_half(wi_sb, 1)
+        copy_half(True, wi_g, 0, bank0)
+        copy_half(False, wi_g, 1, bank1)
+        new_grouped(0)
+        bank0 = transpose_half(x_sb[0], 0)
+        copy_half(True, grouped[0], 0, bank0)
+        quantise(wi_g[:], wi_codes, wi_scales)
+        bank1 = transpose_half(x_sb[0], 1)
+        copy_half(False, grouped[0], 1, bank1)
+        gbi = const.tile([P, 4], F32)
+        nc.vector.tensor_tensor(out=gbi[:], in0=gam[:], in1=pcol[:, 8:12], op=ALU.mult)
+        q1(0)
+        lbank = ps_t.tile([P, 2, 2, P], F32, tag="bank_t")
+        nc.tensor.transpose(lbank[:, 0, 0, :], lam_pad[:], ident[:])
+        lam_rows = const.tile([P, P], F32)
+        nc.vector.tensor_copy(out=lam_rows[:], in_=lbank[:, 0, 0, :])
+        lam_ps = ps_l.tile([P, P], F32)
+        nc.tensor.transpose(lam_ps[:], lam_rows[:], ident[:])
+        new_grouped(1)
+        bank0 = transpose_half(x_sb[1], 0)
+        copy_half(True, grouped[1], 0, bank0)
+        bank1 = transpose_half(x_sb[1], 1)
+        copy_half(False, grouped[1], 1, bank1)
+        q1(1)
+
         bo32 = const.tile([P, FEAT], F32)
+        u_tiles = {}
+        xs_tiles = {}
+        xg = {}
+        x_mx = {}
+        o_tiles = {}
 
-        previous = None
-        for i in range(ROUNDS):
-            x_sb = x_first if i == 0 else load_round(i)
-            in_codes = mxin.tile([P, BLOCK], U32, align_bytes=64, tag="in_codes")
-            in_scales = mxin.tile([P, BLOCK], U8, align_bytes=64, tag="in_scales")
-            transpose_and_quantise(x_sb, in_codes, in_scales)
+        def emit_units(c_blocks, a_blocks):
+            c_units = [(b, jp) for b in c_blocks for jp in range(2)]
+            a_units = [(b, h) for b in a_blocks for h in range(2)]
+            for i in range(max(len(c_units), len(a_units))):
+                banks = []
+                if i < len(c_units):
+                    b, jp = c_units[i]
+                    si, off = where[b]
+                    if si not in u_tiles:
+                        u_sb = upool.tile([P, 4, len(SPANS[si]) * BLOCK], F32, tag="u_sb")
+                        u_tiles[si] = u_sb
+                    for j in (2 * jp, 2 * jp + 1):
+                        u_ps = ps_u.tile([P, BLOCK], F32, tag="u_ps")
+                        nc.tensor.matmul_mx(
+                            out=u_ps[:],
+                            lhsT=wi_codes[:, j * P : (j + 1) * P].bitcast(FP8X4),
+                            lhsT_scale=wi_scales[:, j * P : (j + 1) * P],
+                            rhs=in_mx[b][0][:].bitcast(FP8X4),
+                            rhs_scale=in_mx[b][1][:],
+                            start=True,
+                            stop=True,
+                        )
+                        banks.append((j, u_ps))
+                bank = None
+                if i < len(a_units):
+                    b2, h = a_units[i]
+                    if h == 0:
+                        new_grouped(b2)
+                    bank = transpose_half(x_sb[b2], h)
+                for j, u_ps in banks:
+                    nc.scalar.activation(
+                        out=u_tiles[si][:, j, off : off + BLOCK],
+                        in_=u_ps[:],
+                        func=ACT.Identity,
+                        bias=gbi[:, j : j + 1],
+                        scale=gam[:, j : j + 1],
+                    )
+                if i < len(a_units):
+                    copy_half(True, grouped[b2], h, bank)
 
-            xs = xpool.tile([P, 4, BLOCK], F32, tag="xs")
+        def scan(si):
+            n = len(SPANS[si]) * BLOCK
+            xs = xpool.tile([P, 4, n], F32, tag="xs")
+            xs_tiles[si] = xs
+            first = SPANS[si][0] % BLOCKS_PER_SEQ == 0
             for j in range(4):
-                u_ps = ps_u.tile([P, BLOCK], F32, tag="u_ps")
-                nc.tensor.matmul_mx(
-                    out=u_ps[:],
-                    lhsT=wi_codes[:, j * P : (j + 1) * P].bitcast(FP8X4),
-                    lhsT_scale=wi_scales[:, j * P : (j + 1) * P],
-                    rhs=in_codes[:].bitcast(FP8X4),
-                    rhs_scale=in_scales[:],
-                    start=True,
-                    stop=True,
-                )
-                u_sb = upool.tile([P, BLOCK], F32, tag="u_sb")
-                nc.scalar.activation(
-                    out=u_sb[:], in_=u_ps[:], func=ACT.Identity, bias=gbi[:, j : j + 1], scale=gam[:, j : j + 1]
-                )
-                start_value = 0.0 if i % ROUNDS_PER_SEQ == 0 else previous[:, j, BLOCK - 1 : BLOCK]
+                if first:
+                    start_value = 0.0
+                else:
+                    n_prev = len(SPANS[si - 1]) * BLOCK
+                    start_value = xs_tiles[si - 1][:, j, n_prev - 1 : n_prev]
                 nc.vector.tensor_tensor_scan(
                     out=xs[:, j, :],
-                    data0=lam[:, j : j + 1].to_broadcast([P, BLOCK]),
-                    data1=u_sb[:],
+                    data0=lam_ps[:, j : j + 1].to_broadcast([P, n]),
+                    data1=u_tiles[si][:, j, :],
                     initial=start_value,
                     op0=ALU.mult,
                     op1=ALU.add,
                 )
-            previous = xs
 
-            if i == 0:
-                transpose_and_quantise(wo_sb, wo_codes, wo_scales)
-                nc.vector.tensor_copy(out=bo32[:], in_=bo_bf[:])
+        def regroup(b):
+            si, off = where[b]
+            xg_tile = xgp.tile([P, BLOCK, 4], BF16, align_bytes=64, tag="xg")
+            xg[b] = xg_tile
+            for q in range(2):
+                lo = q * 256
+                nc.gpsimd.tensor_scalar(
+                    out=xg_tile[:, lo : lo + 256, :],
+                    in0=xs_tiles[si][:, :, off + lo : off + lo + 256].rearrange("p j t -> p t j"),
+                    scalar1=1.0,
+                    scalar2=0.0,
+                    op0=ALU.mult,
+                    op1=ALU.add,
+                )
 
-            xg = grp.tile([P, BLOCK, 4], BF16, align_bytes=64, tag="xg")
-            nc.scalar.copy(out=xg[:], in_=xs[:].rearrange("p j t -> p t j"))
+        def q2(b):
             x_codes = mxin.tile([P, BLOCK], U32, align_bytes=64, tag="x_codes")
             x_scales = mxin.tile([P, BLOCK], U8, align_bytes=64, tag="x_scales")
-            nc.vector.quantize_mx(
-                out=x_codes[:].bitcast(FP8X4), scales=x_scales[:], in_=xg[:].rearrange("p t j -> p (t j)")
+            quantise(xg[b][:].rearrange("p t j -> p (t j)"), x_codes, x_scales)
+            x_mx[b] = (x_codes, x_scales)
+
+        def store(b, t0, t1):
+            nc.sync.dma_start(
+                out=out_flat[b * BLOCK + t0 * P : b * BLOCK + t1 * P, :].rearrange("(s p) f -> p s f", p=P),
+                in_=o_tiles[b][:, t0:t1, :],
             )
 
-            o_sb = opool.tile([P, SUB, FEAT], F32, tag="o_sb")
-            for s in range(SUB):
+        def stage2(blocks):
+            g_list = [(b, t) for b in blocks for t in range(4 - G_TILES[b], 4)]
+            v_list = [(b, t) for t in range(4) for b in blocks if t < 4 - G_TILES[b]]
+            order = []
+            iv = 0
+            for k in range(len(g_list)):
+                order.append(g_list[k])
+                order.extend(v_list[iv : iv + 2])
+                iv += 2
+            order.extend(v_list[iv:])
+            for b in blocks:
+                o_sb = opool.tile([P, 4, FEAT], F32, tag="o_sb")
+                o_tiles[b] = o_sb
+            for b, t in order:
                 o_ps = ps_o.tile([P, FEAT], F32, tag="o_ps")
                 nc.tensor.matmul_mx(
                     out=o_ps[:],
-                    lhsT=x_codes[:, s * P : (s + 1) * P].bitcast(FP8X4),
-                    lhsT_scale=x_scales[:, s * P : (s + 1) * P],
+                    lhsT=x_mx[b][0][:, t * P : (t + 1) * P].bitcast(FP8X4),
+                    lhsT_scale=x_mx[b][1][:, t * P : (t + 1) * P],
                     rhs=wo_codes[:].bitcast(FP8X4),
                     rhs_scale=wo_scales[:],
                     start=True,
                     stop=True,
                 )
-                nc.vector.tensor_tensor(out=o_sb[:, s, :], in0=o_ps[:], in1=bo32[:], op=ALU.add)
-            nc.sync.dma_start(
-                out=out_flat[i * BLOCK : (i + 1) * BLOCK, :].rearrange("(s p) f -> p s f", p=P), in_=o_sb[:]
-            )
+                if t < 4 - G_TILES[b]:
+                    nc.vector.tensor_tensor(out=o_tiles[b][:, t, :], in0=o_ps[:], in1=bo32[:], op=ALU.add)
+                else:
+                    nc.scalar.copy(out=o_tiles[b][:, t, :], in_=o_ps[:])
+            for b in blocks:
+                store(b, 0, 4 - G_TILES[b])
+
+        def gp_add(b):
+            for t in range(4 - G_TILES[b], 4):
+                nc.gpsimd.tensor_tensor(out=o_tiles[b][:, t, :], in0=o_tiles[b][:, t, :], in1=bo32[:], op=ALU.add)
+            if G_TILES[b] > 0:
+                store(b, 4 - G_TILES[b], 4)
+
+        for s in range(-1, n_spans + 2):
+            a_blocks = span(s + 2) if s >= 0 else ()
+            emit_units(span(s + 1), a_blocks)
+            if s == 0:
+                wo_g = xgp.tile([P, 4 * BLOCK], BF16, align_bytes=64, tag="xg")
+                for h in range(2):
+                    bank = transpose_half(wo_sb, h)
+                    copy_half(True, wo_g, h, bank)
+                bo_ps = ps_o.tile([P, FEAT], F32, tag="o_ps")
+                nc.tensor.matmul(out=bo_ps[:], lhsT=ones[:], rhs=bo_row[:], start=True, stop=True)
+                nc.scalar.copy(out=bo32[:], in_=bo_ps[:])
+            if 0 <= s < n_spans:
+                scan(s)
+            for b in span(s - 1):
+                regroup(b)
+            for b in span(s - 2):
+                gp_add(b)
+            done = span(s - 1)
+            for k in range(max(len(done), len(a_blocks))):
+                if k < len(done):
+                    q2(done[k])
+                if k < len(a_blocks):
+                    q1(a_blocks[k])
+            if s == 0:
+                quantise(wo_g[:], wo_codes, wo_scales)
+            if len(done) > 0:
+                stage2(done)

@@ -15,11 +15,13 @@ P = 128
 FEAT = 512
 CHAN = 512
 TOKENS = 8192
-BLOCK = 512
-NBLOCKS = TOKENS // BLOCK
-BLOCKS_PER_SEQ = 8
-SPANS = ((0,), (1,), (2, 3), (4, 5), (6, 7), (8, 9), (10, 11), (12, 13), (14,), (15,))
-G_TILES = (1, 1, 1, 2, 1, 2, 1, 2, 1, 2, 1, 2, 1, 2, 1, 0)
+SEQ = 4096
+HALF = 256
+SIZES = (256, 256) + (512,) * 14 + (256, 256)
+STARTS = tuple(sum(SIZES[:b]) for b in range(len(SIZES)))
+GROUPS = ((0,), (1,), (2,), (3, 4), (5, 6), (7, 8), (9, 10), (11, 12), (13, 14), (15,), (16,), (17,))
+G_TILES = (1, 1) + (2,) * 14 + (1, 0)
+ROW_BUFS = 12
 FLOPS = 2 * TOKENS * FEAT * CHAN * 2
 
 
@@ -27,24 +29,30 @@ def tile_slru_t_kernel(tc, inputs, Wi, bi, Wo, bo, params_log, out):
     nc = tc.nc
     x_flat = inputs.flatten_outer_dims()
     out_flat = out.flatten_outer_dims()
-    n_spans = len(SPANS)
+    n_blocks = len(SIZES)
+    n_groups = len(GROUPS)
     where = {}
-    for si in range(n_spans):
-        for k in range(len(SPANS[si])):
-            where[SPANS[si][k]] = (si, k * BLOCK)
+    group_len = []
+    for gi in range(n_groups):
+        off = 0
+        for b in GROUPS[gi]:
+            where[b] = (gi, off)
+            off += SIZES[b]
+        group_len.append(off)
 
-    def span(i):
-        return SPANS[i] if 0 <= i < n_spans else ()
+    def group(i):
+        return GROUPS[i] if 0 <= i < n_groups else ()
 
     with ExitStack() as ctx:
         const = ctx.enter_context(tc.tile_pool(name="const", bufs=1))
-        rows = ctx.enter_context(tc.tile_pool(name="rows", bufs=NBLOCKS + 2))
+        rows = ctx.enter_context(tc.tile_pool(name="rows", bufs=ROW_BUFS))
         grp = ctx.enter_context(tc.tile_pool(name="grp", bufs=2))
         xgp = ctx.enter_context(tc.tile_pool(name="xgp", bufs=3))
         mxin = ctx.enter_context(tc.tile_pool(name="mxin", bufs=3))
         upool = ctx.enter_context(tc.tile_pool(name="upool", bufs=2))
         xpool = ctx.enter_context(tc.tile_pool(name="xpool", bufs=3))
         opool = ctx.enter_context(tc.tile_pool(name="opool", bufs=4))
+        tpool = ctx.enter_context(tc.tile_pool(name="tpool", bufs=3))
         ps_l = ctx.enter_context(tc.psum_pool(name="ps_l", bufs=1))
         ps_t = ctx.enter_context(tc.psum_pool(name="ps_t", bufs=2))
         ps_u = ctx.enter_context(tc.psum_pool(name="ps_u", bufs=2))
@@ -65,30 +73,36 @@ def tile_slru_t_kernel(tc, inputs, Wi, bi, Wo, bo, params_log, out):
         nc.scalar.dma_start(out=prow[4:6, :], in_=bi.rearrange("(u w) -> u w", u=2))
         nc.scalar.dma_start(out=bo_row[0:1, :], in_=bo.rearrange("(o f) -> o f", o=1))
 
+        x_sb = {}
+        loaded = [0]
+
+        def load_next():
+            b = loaded[0]
+            if b >= n_blocks:
+                return
+            loaded[0] = b + 1
+            pieces = SIZES[b] // P
+            x_tile = rows.tile([P, pieces * FEAT], BF16, tag="rows")
+            nc.sync.dma_start(
+                out=x_tile[:].rearrange("p (s h) -> p s h", s=pieces),
+                in_=x_flat[STARTS[b] : STARTS[b] + SIZES[b], :].rearrange("(s p) h -> p s h", p=P),
+            )
+            x_sb[b] = x_tile
+
         wi_sb = rows.tile([P, 4 * FEAT], BF16, tag="rows")
         nc.sync.dma_start(
             out=wi_sb[:].rearrange("p (u e h) -> p u e h", u=2, e=2),
             in_=Wi.rearrange("(u p e) h -> p u e h", u=2, e=2),
         )
-        x_sb = {}
-
-        def load(b):
-            x_tile = rows.tile([P, 4 * FEAT], BF16, tag="rows")
-            nc.sync.dma_start(
-                out=x_tile[:].rearrange("p (s h) -> p s h", s=4),
-                in_=x_flat[b * BLOCK : (b + 1) * BLOCK, :].rearrange("(s p) h -> p s h", p=P),
-            )
-            x_sb[b] = x_tile
-
-        for b in range(3):
-            load(b)
+        for k in range(3):
+            load_next()
         wo_sb = rows.tile([P, 4 * CHAN], BF16, tag="rows")
         nc.sync.dma_start(
             out=wo_sb[:].rearrange("p (a c) -> p a c", a=4),
             in_=Wo.rearrange("(a p) c -> p a c", p=P),
         )
-        for b in range(3, NBLOCKS):
-            load(b)
+        for k in range(ROW_BUFS - 5):
+            load_next()
 
         warm = const.tile([P, 1], F32)
         nc.scalar.activation(out=warm[:], in_=lam_pad[:, 0:1], func=ACT.Exp)
@@ -102,9 +116,9 @@ def tile_slru_t_kernel(tc, inputs, Wi, bi, Wo, bo, params_log, out):
                     nc.tensor.transpose(bank[:, s2, u, :], src32[:, first : first + P], ident[:])
             return bank
 
-        def copy_half(on_scalar, grouped, half, bank):
-            g32 = grouped[:].bitcast(F32).rearrange("p (c u) -> p c u", u=2)
-            dst = g32[:, half * 256 : (half + 1) * 256, :].rearrange("p (s r) u -> p s r u", s=2)
+        def copy_half(on_scalar, g_tile, half, bank):
+            g32 = g_tile[:].bitcast(F32).rearrange("p (c u) -> p c u", u=2)
+            dst = g32[:, half * HALF : (half + 1) * HALF, :].rearrange("p (s r) u -> p s r u", s=2)
             view = bank[:].rearrange("p s u r -> p s r u")
             if on_scalar:
                 nc.scalar.copy(out=dst, in_=view)
@@ -112,84 +126,91 @@ def tile_slru_t_kernel(tc, inputs, Wi, bi, Wo, bo, params_log, out):
                 nc.vector.tensor_copy(out=dst, in_=view)
 
         def quantise(src, codes, scales):
-            nc.vector.quantize_mx(out=codes[:].bitcast(FP8X4), scales=scales[:], in_=src)
+            nc.vector.quantize_mx(out=codes.bitcast(FP8X4), scales=scales, in_=src)
 
         grouped = {}
         in_mx = {}
 
         def new_grouped(b):
-            g_tile = grp.tile([P, 4 * BLOCK], BF16, align_bytes=64, tag="grouped")
+            g_tile = grp.tile([P, 4 * SIZES[b]], BF16, align_bytes=64, tag="grouped")
             grouped[b] = g_tile
 
         def q1(b):
-            in_codes = mxin.tile([P, BLOCK], U32, align_bytes=64, tag="in_codes")
-            in_scales = mxin.tile([P, BLOCK], U8, align_bytes=64, tag="in_scales")
-            quantise(grouped[b][:], in_codes, in_scales)
+            in_codes = mxin.tile([P, SIZES[b]], U32, align_bytes=64, tag="in_codes")
+            in_scales = mxin.tile([P, SIZES[b]], U8, align_bytes=64, tag="in_scales")
+            quantise(grouped[b][:], in_codes[:], in_scales[:])
             in_mx[b] = (in_codes, in_scales)
-
-        pbank = ps_t.tile([P, 2, 2, P], F32, tag="bank_t")
-        nc.tensor.transpose(pbank[:, 0, 0, :], prow[:].bitcast(F32), ident[:])
-        pwords = const.tile([P, 8], F32)
-        nc.vector.tensor_copy(out=pwords[:], in_=pbank[:, 0, 0, 0:8])
-        pcol = pwords[:].bitcast(BF16)
-        nu = const.tile([P, 4], F32)
-        nc.scalar.activation(out=nu[:], in_=pcol[:, 0:4], func=ACT.Exp)
-        nc.scalar.activation(out=lam_pad[:, 0:4], in_=nu[:], func=ACT.Exp, scale=-1.0)
-        gam = const.tile([P, 4], F32)
-        nc.scalar.activation(out=gam[:], in_=pcol[:, 4:8], func=ACT.Exp)
 
         wi_codes = const.tile([P, CHAN], U32, align_bytes=64)
         wi_scales = const.tile([P, CHAN], U8, align_bytes=64)
         wo_codes = const.tile([P, FEAT], U32, align_bytes=64)
         wo_scales = const.tile([P, FEAT], U8, align_bytes=64)
 
-        wi_g = grp.tile([P, 4 * BLOCK], BF16, align_bytes=64, tag="grouped")
-        bank0 = transpose_half(wi_sb, 0)
-        bank1 = transpose_half(wi_sb, 1)
-        copy_half(True, wi_g, 0, bank0)
-        copy_half(False, wi_g, 1, bank1)
+        def quantise_weight_half(g_tile, codes, scales, h):
+            quantise(
+                g_tile[:, h * 4 * HALF : (h + 1) * 4 * HALF],
+                codes[:, h * HALF : (h + 1) * HALF],
+                scales[:, h * HALF : (h + 1) * HALF],
+            )
+
+        wi_g = grp.tile([P, 4 * CHAN], BF16, align_bytes=64, tag="grouped")
+        bank = transpose_half(wi_sb, 0)
+        copy_half(True, wi_g, 0, bank)
         new_grouped(0)
-        bank0 = transpose_half(x_sb[0], 0)
-        copy_half(True, grouped[0], 0, bank0)
-        quantise(wi_g[:], wi_codes, wi_scales)
-        bank1 = transpose_half(x_sb[0], 1)
-        copy_half(False, grouped[0], 1, bank1)
+        bank = transpose_half(x_sb[0], 0)
+        copy_half(False, grouped[0], 0, bank)
+        load_next()
+        pbank = ps_o.tile([P, FEAT], F32, tag="o_ps")
+        nc.tensor.transpose(pbank[:, 0:P], prow[:].bitcast(F32), ident[:])
+        pwords = const.tile([P, 8], F32)
+        nc.vector.tensor_copy(out=pwords[:], in_=pbank[:, 0:8])
+        pcol = pwords[:].bitcast(BF16)
+        nu = const.tile([P, 4], F32)
+        nc.scalar.activation(out=nu[:], in_=pcol[:, 0:4], func=ACT.Exp)
+        nc.scalar.activation(out=lam_pad[:, 0:4], in_=nu[:], func=ACT.Exp, scale=-1.0)
+        gam = const.tile([P, 4], F32)
+        nc.scalar.activation(out=gam[:], in_=pcol[:, 4:8], func=ACT.Exp)
+        bank = transpose_half(wi_sb, 1)
+        copy_half(True, wi_g, 1, bank)
+        load_next()
+        quantise_weight_half(wi_g, wi_codes, wi_scales, 0)
+        q1(0)
         gbi = const.tile([P, 4], F32)
         nc.vector.tensor_tensor(out=gbi[:], in0=gam[:], in1=pcol[:, 8:12], op=ALU.mult)
-        q1(0)
-        lbank = ps_t.tile([P, 2, 2, P], F32, tag="bank_t")
-        nc.tensor.transpose(lbank[:, 0, 0, :], lam_pad[:], ident[:])
+        lbank = ps_o.tile([P, FEAT], F32, tag="o_ps")
+        nc.tensor.transpose(lbank[:, 0:P], lam_pad[:], ident[:])
         lam_rows = const.tile([P, P], F32)
-        nc.vector.tensor_copy(out=lam_rows[:], in_=lbank[:, 0, 0, :])
+        nc.vector.tensor_copy(out=lam_rows[:], in_=lbank[:, 0:P])
         lam_ps = ps_l.tile([P, P], F32)
         nc.tensor.transpose(lam_ps[:], lam_rows[:], ident[:])
+        quantise_weight_half(wi_g, wi_codes, wi_scales, 1)
         new_grouped(1)
-        bank0 = transpose_half(x_sb[1], 0)
-        copy_half(True, grouped[1], 0, bank0)
-        bank1 = transpose_half(x_sb[1], 1)
-        copy_half(False, grouped[1], 1, bank1)
+        bank = transpose_half(x_sb[1], 0)
+        copy_half(False, grouped[1], 0, bank)
+        load_next()
         q1(1)
 
         bo32 = const.tile([P, FEAT], F32)
         u_tiles = {}
         xs_tiles = {}
+        tokens = {}
         xg = {}
         x_mx = {}
         o_tiles = {}
 
         def emit_units(c_blocks, a_blocks):
             c_units = [(b, jp) for b in c_blocks for jp in range(2)]
-            a_units = [(b, h) for b in a_blocks for h in range(2)]
+            a_units = [(b, h) for b in a_blocks for h in range(SIZES[b] // HALF)]
             for i in range(max(len(c_units), len(a_units))):
                 banks = []
                 if i < len(c_units):
                     b, jp = c_units[i]
-                    si, off = where[b]
-                    if si not in u_tiles:
-                        u_sb = upool.tile([P, 4, len(SPANS[si]) * BLOCK], F32, tag="u_sb")
-                        u_tiles[si] = u_sb
+                    gi, off = where[b]
+                    if gi not in u_tiles:
+                        u_sb = upool.tile([P, 4, group_len[gi]], F32, tag="u_sb")
+                        u_tiles[gi] = u_sb
                     for j in (2 * jp, 2 * jp + 1):
-                        u_ps = ps_u.tile([P, BLOCK], F32, tag="u_ps")
+                        u_ps = ps_u.tile([P, SIZES[b]], F32, tag="u_ps")
                         nc.tensor.matmul_mx(
                             out=u_ps[:],
                             lhsT=wi_codes[:, j * P : (j + 1) * P].bitcast(FP8X4),
@@ -200,82 +221,92 @@ def tile_slru_t_kernel(tc, inputs, Wi, bi, Wo, bo, params_log, out):
                             stop=True,
                         )
                         banks.append((j, u_ps))
-                bank = None
+                bank_a = None
                 if i < len(a_units):
                     b2, h = a_units[i]
                     if h == 0:
                         new_grouped(b2)
-                    bank = transpose_half(x_sb[b2], h)
+                    bank_a = transpose_half(x_sb[b2], h)
+                    if h == SIZES[b2] // HALF - 1:
+                        load_next()
                 for j, u_ps in banks:
                     nc.scalar.activation(
-                        out=u_tiles[si][:, j, off : off + BLOCK],
+                        out=u_tiles[gi][:, j, off : off + SIZES[b]],
                         in_=u_ps[:],
                         func=ACT.Identity,
                         bias=gbi[:, j : j + 1],
                         scale=gam[:, j : j + 1],
                     )
                 if i < len(a_units):
-                    copy_half(True, grouped[b2], h, bank)
+                    copy_half(True, grouped[b2], h, bank_a)
 
-        def scan(si):
-            n = len(SPANS[si]) * BLOCK
+        def scan(gi):
+            n = group_len[gi]
             xs = xpool.tile([P, 4, n], F32, tag="xs")
-            xs_tiles[si] = xs
-            first = SPANS[si][0] % BLOCKS_PER_SEQ == 0
+            xs_tiles[gi] = xs
+            first = STARTS[GROUPS[gi][0]] % SEQ == 0
             for j in range(4):
                 if first:
                     start_value = 0.0
                 else:
-                    n_prev = len(SPANS[si - 1]) * BLOCK
-                    start_value = xs_tiles[si - 1][:, j, n_prev - 1 : n_prev]
+                    n_prev = group_len[gi - 1]
+                    start_value = xs_tiles[gi - 1][:, j, n_prev - 1 : n_prev]
                 nc.vector.tensor_tensor_scan(
                     out=xs[:, j, :],
                     data0=lam_ps[:, j : j + 1].to_broadcast([P, n]),
-                    data1=u_tiles[si][:, j, :],
+                    data1=u_tiles[gi][:, j, :],
                     initial=start_value,
                     op0=ALU.mult,
                     op1=ALU.add,
                 )
 
         def regroup(b):
-            si, off = where[b]
-            xg_tile = xgp.tile([P, BLOCK, 4], BF16, align_bytes=64, tag="xg")
+            gi, off = where[b]
+            n = SIZES[b]
+            xg_tile = xgp.tile([P, n, 4], BF16, align_bytes=64, tag="xg")
             xg[b] = xg_tile
-            for q in range(2):
-                lo = q * 256
-                nc.gpsimd.tensor_scalar(
-                    out=xg_tile[:, lo : lo + 256, :],
-                    in0=xs_tiles[si][:, :, off + lo : off + lo + 256].rearrange("p j t -> p t j"),
-                    scalar1=1.0,
-                    scalar2=0.0,
-                    op0=ALU.mult,
-                    op1=ALU.add,
+            n_g = n // 2 if b == n_blocks - 1 else n
+            nc.gpsimd.tensor_scalar(
+                out=xg_tile[:, 0:n_g, :],
+                in0=xs_tiles[gi][:, :, off : off + n_g].rearrange("p j t -> p t j"),
+                scalar1=tokens[gi][:, 0:1],
+                scalar2=0.0,
+                op0=ALU.mult,
+                op1=ALU.add,
+            )
+            if n_g < n:
+                nc.scalar.copy(
+                    out=xg_tile[:, n_g:n, :],
+                    in_=xs_tiles[gi][:, :, off + n_g : off + n].rearrange("p j t -> p t j"),
                 )
 
         def q2(b):
-            x_codes = mxin.tile([P, BLOCK], U32, align_bytes=64, tag="x_codes")
-            x_scales = mxin.tile([P, BLOCK], U8, align_bytes=64, tag="x_scales")
-            quantise(xg[b][:].rearrange("p t j -> p (t j)"), x_codes, x_scales)
+            x_codes = mxin.tile([P, SIZES[b]], U32, align_bytes=64, tag="x_codes")
+            x_scales = mxin.tile([P, SIZES[b]], U8, align_bytes=64, tag="x_scales")
+            quantise(xg[b][:].rearrange("p t j -> p (t j)"), x_codes[:], x_scales[:])
             x_mx[b] = (x_codes, x_scales)
 
         def store(b, t0, t1):
             nc.sync.dma_start(
-                out=out_flat[b * BLOCK + t0 * P : b * BLOCK + t1 * P, :].rearrange("(s p) f -> p s f", p=P),
+                out=out_flat[STARTS[b] + t0 * P : STARTS[b] + t1 * P, :].rearrange("(s p) f -> p s f", p=P),
                 in_=o_tiles[b][:, t0:t1, :],
             )
 
+        def v_tiles(b):
+            return SIZES[b] // P - G_TILES[b]
+
         def stage2(blocks):
-            g_list = [(b, t) for b in blocks for t in range(4 - G_TILES[b], 4)]
-            v_list = [(b, t) for t in range(4) for b in blocks if t < 4 - G_TILES[b]]
+            g_list = [(b, t) for b in blocks for t in range(v_tiles(b), SIZES[b] // P)]
+            v_list = [(b, t) for t in range(4) for b in blocks if t < v_tiles(b)]
             order = []
             iv = 0
             for k in range(len(g_list)):
                 order.append(g_list[k])
-                order.extend(v_list[iv : iv + 2])
-                iv += 2
+                order.extend(v_list[iv : iv + 1])
+                iv += 1
             order.extend(v_list[iv:])
             for b in blocks:
-                o_sb = opool.tile([P, 4, FEAT], F32, tag="o_sb")
+                o_sb = opool.tile([P, SIZES[b] // P, FEAT], F32, tag="o_sb")
                 o_tiles[b] = o_sb
             for b, t in order:
                 o_ps = ps_o.tile([P, FEAT], F32, tag="o_ps")
@@ -288,43 +319,48 @@ def tile_slru_t_kernel(tc, inputs, Wi, bi, Wo, bo, params_log, out):
                     start=True,
                     stop=True,
                 )
-                if t < 4 - G_TILES[b]:
+                if t < v_tiles(b):
                     nc.vector.tensor_tensor(out=o_tiles[b][:, t, :], in0=o_ps[:], in1=bo32[:], op=ALU.add)
                 else:
                     nc.scalar.copy(out=o_tiles[b][:, t, :], in_=o_ps[:])
             for b in blocks:
-                store(b, 0, 4 - G_TILES[b])
+                store(b, 0, v_tiles(b))
 
         def gp_add(b):
-            for t in range(4 - G_TILES[b], 4):
+            for t in range(v_tiles(b), SIZES[b] // P):
                 nc.gpsimd.tensor_tensor(out=o_tiles[b][:, t, :], in0=o_tiles[b][:, t, :], in1=bo32[:], op=ALU.add)
             if G_TILES[b] > 0:
-                store(b, 4 - G_TILES[b], 4)
+                store(b, v_tiles(b), SIZES[b] // P)
 
-        for s in range(-1, n_spans + 2):
-            a_blocks = span(s + 2) if s >= 0 else ()
-            emit_units(span(s + 1), a_blocks)
+        for s in range(-1, n_groups + 2):
+            a_blocks = group(s + 2) if s >= 0 else ()
+            emit_units(group(s + 1), a_blocks)
             if s == 0:
-                wo_g = xgp.tile([P, 4 * BLOCK], BF16, align_bytes=64, tag="xg")
+                wo_g = xgp.tile([P, 4 * FEAT], BF16, align_bytes=64, tag="xg")
                 for h in range(2):
                     bank = transpose_half(wo_sb, h)
                     copy_half(True, wo_g, h, bank)
+                load_next()
                 bo_ps = ps_o.tile([P, FEAT], F32, tag="o_ps")
                 nc.tensor.matmul(out=bo_ps[:], lhsT=ones[:], rhs=bo_row[:], start=True, stop=True)
                 nc.scalar.copy(out=bo32[:], in_=bo_ps[:])
-            if 0 <= s < n_spans:
+            if 0 <= s < n_groups:
                 scan(s)
-            for b in span(s - 1):
+            for b in group(s - 1):
                 regroup(b)
-            for b in span(s - 2):
+            for b in group(s - 2):
                 gp_add(b)
-            done = span(s - 1)
+            done = group(s - 1)
             for k in range(max(len(done), len(a_blocks))):
                 if k < len(done):
                     q2(done[k])
                 if k < len(a_blocks):
                     q1(a_blocks[k])
             if s == 0:
-                quantise(wo_g[:], wo_codes, wo_scales)
+                quantise(wo_g[:], wo_codes[:], wo_scales[:])
+            if 0 <= s < n_groups:
+                token = tpool.tile([P, 1], F32, tag="token")
+                nc.vector.memset(token[:], 1.0)
+                tokens[s] = token
             if len(done) > 0:
                 stage2(done)

@@ -54,9 +54,7 @@ def tile_slru_t_kernel(tc, inputs, Wi, bi, Wo, bo, params_log, out):
         opool = ctx.enter_context(tc.tile_pool(name="opool", bufs=4))
         tpool = ctx.enter_context(tc.tile_pool(name="tpool", bufs=3))
         ps_l = ctx.enter_context(tc.psum_pool(name="ps_l", bufs=1))
-        ps_t = ctx.enter_context(tc.psum_pool(name="ps_t", bufs=2))
-        ps_u = ctx.enter_context(tc.psum_pool(name="ps_u", bufs=2))
-        ps_o = ctx.enter_context(tc.psum_pool(name="ps_o", bufs=3))
+        ps = ctx.enter_context(tc.psum_pool(name="ps", bufs=7))
         ctx.enter_context(tc.manual_schedule())
 
         ident = const.tile([P, P], F32)
@@ -108,7 +106,7 @@ def tile_slru_t_kernel(tc, inputs, Wi, bi, Wo, bo, params_log, out):
         nc.scalar.activation(out=warm[:], in_=lam_pad[:, 0:1], func=ACT.Exp)
 
         def transpose_half(src, half):
-            bank = ps_t.tile([P, 2, 2, P], F32, tag="bank_t")
+            bank = ps.tile([P, 2, 2, P], F32, tag="bank")
             src32 = src[:].bitcast(F32)
             for s2 in range(2):
                 for u in range(2):
@@ -160,7 +158,7 @@ def tile_slru_t_kernel(tc, inputs, Wi, bi, Wo, bo, params_log, out):
         bank = transpose_half(x_sb[0], 0)
         copy_half(False, grouped[0], 0, bank)
         load_next()
-        pbank = ps_o.tile([P, FEAT], F32, tag="o_ps")
+        pbank = ps.tile([P, FEAT], F32, tag="bank")
         nc.tensor.transpose(pbank[:, 0:P], prow[:].bitcast(F32), ident[:])
         pwords = const.tile([P, 8], F32)
         nc.vector.tensor_copy(out=pwords[:], in_=pbank[:, 0:8])
@@ -177,7 +175,7 @@ def tile_slru_t_kernel(tc, inputs, Wi, bi, Wo, bo, params_log, out):
         q1(0)
         gbi = const.tile([P, 4], F32)
         nc.vector.tensor_tensor(out=gbi[:], in0=gam[:], in1=pcol[:, 8:12], op=ALU.mult)
-        lbank = ps_o.tile([P, FEAT], F32, tag="o_ps")
+        lbank = ps.tile([P, FEAT], F32, tag="bank")
         nc.tensor.transpose(lbank[:, 0:P], lam_pad[:], ident[:])
         lam_rows = const.tile([P, P], F32)
         nc.vector.tensor_copy(out=lam_rows[:], in_=lbank[:, 0:P])
@@ -210,7 +208,7 @@ def tile_slru_t_kernel(tc, inputs, Wi, bi, Wo, bo, params_log, out):
                         u_sb = upool.tile([P, 4, group_len[gi]], F32, tag="u_sb")
                         u_tiles[gi] = u_sb
                     for j in (2 * jp, 2 * jp + 1):
-                        u_ps = ps_u.tile([P, SIZES[b]], F32, tag="u_ps")
+                        u_ps = ps.tile([P, SIZES[b]], F32, tag="bank")
                         nc.tensor.matmul_mx(
                             out=u_ps[:],
                             lhsT=wi_codes[:, j * P : (j + 1) * P].bitcast(FP8X4),
@@ -296,20 +294,15 @@ def tile_slru_t_kernel(tc, inputs, Wi, bi, Wo, bo, params_log, out):
             return SIZES[b] // P - G_TILES[b]
 
         def stage2(blocks):
-            g_list = [(b, t) for b in blocks for t in range(v_tiles(b), SIZES[b] // P)]
-            v_list = [(b, t) for t in range(4) for b in blocks if t < v_tiles(b)]
             order = []
-            iv = 0
-            for k in range(len(g_list)):
-                order.append(g_list[k])
-                order.extend(v_list[iv : iv + 1])
-                iv += 1
-            order.extend(v_list[iv:])
+            for b in blocks:
+                order.extend([(b, t) for t in range(v_tiles(b), SIZES[b] // P)])
+                order.extend([(b, t) for t in range(v_tiles(b))])
             for b in blocks:
                 o_sb = opool.tile([P, SIZES[b] // P, FEAT], F32, tag="o_sb")
                 o_tiles[b] = o_sb
             for b, t in order:
-                o_ps = ps_o.tile([P, FEAT], F32, tag="o_ps")
+                o_ps = ps.tile([P, FEAT], F32, tag="bank")
                 nc.tensor.matmul_mx(
                     out=o_ps[:],
                     lhsT=x_mx[b][0][:, t * P : (t + 1) * P].bitcast(FP8X4),
@@ -341,7 +334,7 @@ def tile_slru_t_kernel(tc, inputs, Wi, bi, Wo, bo, params_log, out):
                     bank = transpose_half(wo_sb, h)
                     copy_half(True, wo_g, h, bank)
                 load_next()
-                bo_ps = ps_o.tile([P, FEAT], F32, tag="o_ps")
+                bo_ps = ps.tile([P, FEAT], F32, tag="bank")
                 nc.tensor.matmul(out=bo_ps[:], lhsT=ones[:], rhs=bo_row[:], start=True, stop=True)
                 nc.scalar.copy(out=bo32[:], in_=bo_ps[:])
             if 0 <= s < n_groups:
@@ -351,11 +344,10 @@ def tile_slru_t_kernel(tc, inputs, Wi, bi, Wo, bo, params_log, out):
             for b in group(s - 2):
                 gp_add(b)
             done = group(s - 1)
-            for k in range(max(len(done), len(a_blocks))):
-                if k < len(done):
-                    q2(done[k])
-                if k < len(a_blocks):
-                    q1(a_blocks[k])
+            for b in done:
+                q2(b)
+            for b in a_blocks:
+                q1(b)
             if s == 0:
                 quantise(wo_g[:], wo_codes[:], wo_scales[:])
             if 0 <= s < n_groups:

@@ -20,7 +20,7 @@ HALF = 256
 SIZES = (256, 256) + (512,) * 14 + (256, 256)
 STARTS = tuple(sum(SIZES[:b]) for b in range(len(SIZES)))
 GROUPS = ((0,), (1,), (2,), (3, 4), (5, 6), (7, 8), (9, 10), (11, 12), (13, 14), (15,), (16,), (17,))
-G_TILES = (1, 1) + (2,) * 14 + (1, 0)
+G_TILES = (1, 1, 2) + (2, 3) * 6 + (2, 1, 0)
 ROW_BUFS = 12
 FLOPS = 2 * TOKENS * FEAT * CHAN * 2
 
@@ -52,7 +52,6 @@ def tile_slru_t_kernel(tc, inputs, Wi, bi, Wo, bo, params_log, out):
         upool = ctx.enter_context(tc.tile_pool(name="upool", bufs=2))
         xpool = ctx.enter_context(tc.tile_pool(name="xpool", bufs=3))
         opool = ctx.enter_context(tc.tile_pool(name="opool", bufs=4))
-        tpool = ctx.enter_context(tc.tile_pool(name="tpool", bufs=3))
         ps_l = ctx.enter_context(tc.psum_pool(name="ps_l", bufs=1))
         ps = ctx.enter_context(tc.psum_pool(name="ps", bufs=7))
         ctx.enter_context(tc.manual_schedule())
@@ -191,43 +190,44 @@ def tile_slru_t_kernel(tc, inputs, Wi, bi, Wo, bo, params_log, out):
         bo32 = const.tile([P, FEAT], F32)
         u_tiles = {}
         xs_tiles = {}
-        tokens = {}
         xg = {}
         x_mx = {}
         o_tiles = {}
 
-        def emit_units(c_blocks, a_blocks):
-            c_units = [(b, jp) for b in c_blocks for jp in range(2)]
-            a_units = [(b, h) for b in a_blocks for h in range(SIZES[b] // HALF)]
-            for i in range(max(len(c_units), len(a_units))):
-                banks = []
-                if i < len(c_units):
-                    b, jp = c_units[i]
-                    gi, off = where[b]
-                    if gi not in u_tiles:
-                        u_sb = upool.tile([P, 4, group_len[gi]], F32, tag="u_sb")
-                        u_tiles[gi] = u_sb
-                    for j in (2 * jp, 2 * jp + 1):
-                        u_ps = ps.tile([P, SIZES[b]], F32, tag="bank")
-                        nc.tensor.matmul_mx(
-                            out=u_ps[:],
-                            lhsT=wi_codes[:, j * P : (j + 1) * P].bitcast(FP8X4),
-                            lhsT_scale=wi_scales[:, j * P : (j + 1) * P],
-                            rhs=in_mx[b][0][:].bitcast(FP8X4),
-                            rhs_scale=in_mx[b][1][:],
-                            start=True,
-                            stop=True,
-                        )
-                        banks.append((j, u_ps))
-                bank_a = None
-                if i < len(a_units):
-                    b2, h = a_units[i]
-                    if h == 0:
-                        new_grouped(b2)
+        def s_share(gi):
+            if gi == n_groups - 1:
+                return group_len[gi] // 2
+            return group_len[gi] // 4 if group_len[gi] >= 512 else 0
+
+        def phase1(c_blocks, a_blocks, r_gi):
+            for b2 in a_blocks:
+                new_grouped(b2)
+                for h in range(SIZES[b2] // HALF):
                     bank_a = transpose_half(x_sb[b2], h)
-                    if h == SIZES[b2] // HALF - 1:
-                        load_next()
-                for j, u_ps in banks:
+                    copy_half(True, grouped[b2], h, bank_a)
+                load_next()
+            if 0 <= r_gi < n_groups and s_share(r_gi) > 0:
+                n = group_len[r_gi]
+                lo = n - s_share(r_gi)
+                nc.scalar.copy(
+                    out=xg[r_gi][:, lo:n, :], in_=xs_tiles[r_gi][:, :, lo:n].rearrange("p j t -> p t j")
+                )
+            for b in c_blocks:
+                gi, off = where[b]
+                if gi not in u_tiles:
+                    u_sb = upool.tile([P, 4, group_len[gi]], F32, tag="u_sb")
+                    u_tiles[gi] = u_sb
+                for j in range(4):
+                    u_ps = ps.tile([P, SIZES[b]], F32, tag="bank")
+                    nc.tensor.matmul_mx(
+                        out=u_ps[:],
+                        lhsT=wi_codes[:, j * P : (j + 1) * P].bitcast(FP8X4),
+                        lhsT_scale=wi_scales[:, j * P : (j + 1) * P],
+                        rhs=in_mx[b][0][:].bitcast(FP8X4),
+                        rhs_scale=in_mx[b][1][:],
+                        start=True,
+                        stop=True,
+                    )
                     nc.scalar.activation(
                         out=u_tiles[gi][:, j, off : off + SIZES[b]],
                         in_=u_ps[:],
@@ -235,8 +235,6 @@ def tile_slru_t_kernel(tc, inputs, Wi, bi, Wo, bo, params_log, out):
                         bias=gbi[:, j : j + 1],
                         scale=gam[:, j : j + 1],
                     )
-                if i < len(a_units):
-                    copy_half(True, grouped[b2], h, bank_a)
 
         def scan(gi):
             n = group_len[gi]
@@ -258,30 +256,22 @@ def tile_slru_t_kernel(tc, inputs, Wi, bi, Wo, bo, params_log, out):
                     op1=ALU.add,
                 )
 
-        def regroup(b):
-            gi, off = where[b]
-            n = SIZES[b]
-            xg_tile = xgp.tile([P, n, 4], BF16, align_bytes=64, tag="xg")
-            xg[b] = xg_tile
-            n_g = n // 2 if b == n_blocks - 1 else n
+        def regroup(gi):
+            n_g = group_len[gi] - s_share(gi)
             nc.gpsimd.tensor_scalar(
-                out=xg_tile[:, 0:n_g, :],
-                in0=xs_tiles[gi][:, :, off : off + n_g].rearrange("p j t -> p t j"),
-                scalar1=tokens[gi][:, 0:1],
+                out=xg[gi][:, 0:n_g, :],
+                in0=xs_tiles[gi][:, :, 0:n_g].rearrange("p j t -> p t j"),
+                scalar1=1.0,
                 scalar2=0.0,
                 op0=ALU.mult,
                 op1=ALU.add,
             )
-            if n_g < n:
-                nc.scalar.copy(
-                    out=xg_tile[:, n_g:n, :],
-                    in_=xs_tiles[gi][:, :, off + n_g : off + n].rearrange("p j t -> p t j"),
-                )
 
         def q2(b):
             x_codes = mxin.tile([P, SIZES[b]], U32, align_bytes=64, tag="x_codes")
             x_scales = mxin.tile([P, SIZES[b]], U8, align_bytes=64, tag="x_scales")
-            quantise(xg[b][:].rearrange("p t j -> p (t j)"), x_codes[:], x_scales[:])
+            gi, off = where[b]
+            quantise(xg[gi][:, off : off + SIZES[b], :].rearrange("p t j -> p (t j)"), x_codes[:], x_scales[:])
             x_mx[b] = (x_codes, x_scales)
 
         def store(b, t0, t1):
@@ -296,8 +286,9 @@ def tile_slru_t_kernel(tc, inputs, Wi, bi, Wo, bo, params_log, out):
         def stage2(blocks):
             order = []
             for b in blocks:
-                order.extend([(b, t) for t in range(v_tiles(b), SIZES[b] // P)])
                 order.extend([(b, t) for t in range(v_tiles(b))])
+            for b in blocks:
+                order.extend([(b, t) for t in range(v_tiles(b), SIZES[b] // P)])
             for b in blocks:
                 o_sb = opool.tile([P, SIZES[b] // P, FEAT], F32, tag="o_sb")
                 o_tiles[b] = o_sb
@@ -320,14 +311,16 @@ def tile_slru_t_kernel(tc, inputs, Wi, bi, Wo, bo, params_log, out):
                 store(b, 0, v_tiles(b))
 
         def gp_add(b):
-            for t in range(v_tiles(b), SIZES[b] // P):
-                nc.gpsimd.tensor_tensor(out=o_tiles[b][:, t, :], in0=o_tiles[b][:, t, :], in1=bo32[:], op=ALU.add)
             if G_TILES[b] > 0:
+                part = o_tiles[b][:, v_tiles(b) : SIZES[b] // P, :]
+                nc.gpsimd.tensor_tensor(
+                    out=part, in0=part, in1=bo32[:].unsqueeze(1).to_broadcast([P, G_TILES[b], FEAT]), op=ALU.add
+                )
                 store(b, v_tiles(b), SIZES[b] // P)
 
         for s in range(-1, n_groups + 2):
             a_blocks = group(s + 2) if s >= 0 else ()
-            emit_units(group(s + 1), a_blocks)
+            phase1(group(s + 1), a_blocks, s - 1)
             if s == 0:
                 wo_g = xgp.tile([P, 4 * FEAT], BF16, align_bytes=64, tag="xg")
                 for h in range(2):
@@ -339,8 +332,8 @@ def tile_slru_t_kernel(tc, inputs, Wi, bi, Wo, bo, params_log, out):
                 nc.scalar.copy(out=bo32[:], in_=bo_ps[:])
             if 0 <= s < n_groups:
                 scan(s)
-            for b in group(s - 1):
-                regroup(b)
+            if 0 <= s - 1 < n_groups:
+                regroup(s - 1)
             for b in group(s - 2):
                 gp_add(b)
             done = group(s - 1)
@@ -351,8 +344,8 @@ def tile_slru_t_kernel(tc, inputs, Wi, bi, Wo, bo, params_log, out):
             if s == 0:
                 quantise(wo_g[:], wo_codes[:], wo_scales[:])
             if 0 <= s < n_groups:
-                token = tpool.tile([P, 1], F32, tag="token")
-                nc.vector.memset(token[:], 1.0)
-                tokens[s] = token
+                xg_tile = xgp.tile([P, group_len[s], 4], BF16, align_bytes=64, tag="xg")
+                nc.vector.memset(xg_tile[:].rearrange("p t j -> p (t j)")[:, 0:2].bitcast(F32), 0.0)
+                xg[s] = xg_tile
             if len(done) > 0:
                 stage2(done)

@@ -20,7 +20,8 @@ HALF = 256
 SIZES = (256, 256) + (512,) * 14 + (256, 256)
 STARTS = tuple(sum(SIZES[:b]) for b in range(len(SIZES)))
 GROUPS = ((0,), (1,), (2,), (3, 4), (5, 6), (7, 8), (9, 10), (11, 12), (13, 14), (15,), (16,), (17,))
-G_TILES = (1, 1, 2) + (2, 3) * 6 + (2, 1, 0)
+G_TILES = (1, 1, 2) + (2, 3) * 4 + (2, 2) * 2 + (2, 0, 0)
+S_SHARE = (0, 0, 128, 256, 256, 256, 256, 256, 768, 512, 256, 256)
 ROW_BUFS = 12
 FLOPS = 2 * TOKENS * FEAT * CHAN * 2
 
@@ -194,24 +195,13 @@ def tile_slru_t_kernel(tc, inputs, Wi, bi, Wo, bo, params_log, out):
         x_mx = {}
         o_tiles = {}
 
-        def s_share(gi):
-            if gi == n_groups - 1:
-                return group_len[gi] // 2
-            return group_len[gi] // 4 if group_len[gi] >= 512 else 0
-
-        def phase1(c_blocks, a_blocks, r_gi):
+        def phase1(c_blocks, a_blocks):
             for b2 in a_blocks:
                 new_grouped(b2)
                 for h in range(SIZES[b2] // HALF):
                     bank_a = transpose_half(x_sb[b2], h)
                     copy_half(True, grouped[b2], h, bank_a)
                 load_next()
-            if 0 <= r_gi < n_groups and s_share(r_gi) > 0:
-                n = group_len[r_gi]
-                lo = n - s_share(r_gi)
-                nc.scalar.copy(
-                    out=xg[r_gi][:, lo:n, :], in_=xs_tiles[r_gi][:, :, lo:n].rearrange("p j t -> p t j")
-                )
             for b in c_blocks:
                 gi, off = where[b]
                 if gi not in u_tiles:
@@ -256,16 +246,23 @@ def tile_slru_t_kernel(tc, inputs, Wi, bi, Wo, bo, params_log, out):
                     op1=ALU.add,
                 )
 
-        def regroup(gi):
-            n_g = group_len[gi] - s_share(gi)
-            nc.gpsimd.tensor_scalar(
-                out=xg[gi][:, 0:n_g, :],
-                in0=xs_tiles[gi][:, :, 0:n_g].rearrange("p j t -> p t j"),
-                scalar1=1.0,
-                scalar2=0.0,
-                op0=ALU.mult,
-                op1=ALU.add,
-            )
+        def regroup_scalar(gi):
+            n = group_len[gi]
+            lo = n - S_SHARE[gi]
+            if lo < n:
+                nc.scalar.copy(out=xg[gi][:, lo:n, :], in_=xs_tiles[gi][:, :, lo:n].rearrange("p j t -> p t j"))
+
+        def regroup_gpsimd(gi):
+            n_g = group_len[gi] - S_SHARE[gi]
+            if n_g > 0:
+                nc.gpsimd.tensor_scalar(
+                    out=xg[gi][:, 0:n_g, :],
+                    in0=xs_tiles[gi][:, :, 0:n_g].rearrange("p j t -> p t j"),
+                    scalar1=1.0,
+                    scalar2=0.0,
+                    op0=ALU.mult,
+                    op1=ALU.add,
+                )
 
         def q2(b):
             x_codes = mxin.tile([P, SIZES[b]], U32, align_bytes=64, tag="x_codes")
@@ -320,7 +317,7 @@ def tile_slru_t_kernel(tc, inputs, Wi, bi, Wo, bo, params_log, out):
 
         for s in range(-1, n_groups + 2):
             a_blocks = group(s + 2) if s >= 0 else ()
-            phase1(group(s + 1), a_blocks, s - 1)
+            phase1(group(s + 1), a_blocks)
             if s == 0:
                 wo_g = xgp.tile([P, 4 * FEAT], BF16, align_bytes=64, tag="xg")
                 for h in range(2):
@@ -332,20 +329,21 @@ def tile_slru_t_kernel(tc, inputs, Wi, bi, Wo, bo, params_log, out):
                 nc.scalar.copy(out=bo32[:], in_=bo_ps[:])
             if 0 <= s < n_groups:
                 scan(s)
+                xg_tile = xgp.tile([P, group_len[s], 4], BF16, align_bytes=64, tag="xg")
+                xg[s] = xg_tile
+                regroup_scalar(s)
             if 0 <= s - 1 < n_groups:
-                regroup(s - 1)
+                regroup_gpsimd(s - 1)
             for b in group(s - 2):
                 gp_add(b)
             done = group(s - 1)
+            if s == 1:
+                quantise(wo_g[:], wo_codes[:], wo_scales[:])
             for b in done:
                 q2(b)
             for b in a_blocks:
                 q1(b)
-            if s == 0:
-                quantise(wo_g[:], wo_codes[:], wo_scales[:])
-            if 0 <= s < n_groups:
-                xg_tile = xgp.tile([P, group_len[s], 4], BF16, align_bytes=64, tag="xg")
-                nc.vector.memset(xg_tile[:].rearrange("p t j -> p (t j)")[:, 0:2].bitcast(F32), 0.0)
-                xg[s] = xg_tile
+            if 0 <= s < n_groups and S_SHARE[s] < group_len[s]:
+                nc.vector.memset(xg[s][:].rearrange("p t j -> p (t j)")[:, 0:2].bitcast(F32), 0.0)
             if len(done) > 0:
                 stage2(done)

@@ -20,8 +20,8 @@ HALF = 256
 SIZES = (256, 256) + (512,) * 14 + (256, 256)
 STARTS = tuple(sum(SIZES[:b]) for b in range(len(SIZES)))
 GROUPS = ((0,), (1,), (2,), (3, 4), (5, 6), (7, 8), (9, 10), (11, 12), (13, 14), (15,), (16,), (17,))
-G_TILES = (1, 1, 2) + (2, 3) * 4 + (2, 2) * 2 + (2, 0, 0)
-S_SHARE = (0, 0, 128, 256, 256, 256, 256, 256, 768, 512, 256, 256)
+G_TILES = (1, 1, 2) + (3, 3) * 4 + (2, 2) * 2 + (2, 0, 0)
+S_SHARE = (0, 0, 128, 512, 512, 512, 512, 512, 768, 512, 256, 256)
 ROW_BUFS = 12
 FLOPS = 2 * TOKENS * FEAT * CHAN * 2
 
@@ -250,7 +250,10 @@ def tile_slru_t_kernel(tc, inputs, Wi, bi, Wo, bo, params_log, out):
             n = group_len[gi]
             lo = n - S_SHARE[gi]
             if lo < n:
-                nc.scalar.copy(out=xg[gi][:, lo:n, :], in_=xs_tiles[gi][:, :, lo:n].rearrange("p j t -> p t j"))
+                nc.scalar.copy(
+                    out=xg[gi][:, lo:n, :].rearrange("p (c i) j -> p c j i", i=4),
+                    in_=xs_tiles[gi][:, :, lo:n].rearrange("p j (c i) -> p c j i", i=4),
+                )
 
         def regroup_gpsimd(gi):
             n_g = group_len[gi] - S_SHARE[gi]

@@ -17,11 +17,11 @@ CHAN = 512
 TOKENS = 8192
 SEQ = 4096
 HALF = 256
-SIZES = (256, 256) + (512,) * 14 + (256, 256)
+SIZES = (256, 256) + (512,) * 15
 STARTS = tuple(sum(SIZES[:b]) for b in range(len(SIZES)))
-GROUPS = ((0,), (1,), (2,), (3, 4), (5, 6), (7, 8), (9, 10), (11, 12), (13, 14), (15,), (16,), (17,))
-G_TILES = (1, 1, 2) + (3, 3) * 4 + (2, 2) * 2 + (2, 0, 0)
-S_SHARE = (0, 0, 128, 512, 512, 512, 512, 512, 768, 512, 256, 256)
+GROUPS = ((0,), (1,), (2,), (3, 4), (5, 6), (7, 8), (9, 10), (11, 12), (13, 14), (15,), (16,))
+G_TILES = (1, 1, 2) + (3, 3) * 4 + (2, 2) * 2 + (2, 0)
+S_SHARE = (0, 0, 128, 512, 512, 512, 512, 512, 768, 512, 384)
 ROW_BUFS = 12
 FLOPS = 2 * TOKENS * FEAT * CHAN * 2
 
@@ -88,12 +88,13 @@ def tile_slru_t_kernel(tc, inputs, Wi, bi, Wo, bo, params_log, out):
             x_sb[b] = x_tile
 
         wi_sb = rows.tile([P, 4 * FEAT], BF16, tag="rows")
-        nc.sync.dma_start(
-            out=wi_sb[:].rearrange("p (u e h) -> p u e h", u=2, e=2),
-            in_=Wi.rearrange("(u p e) h -> p u e h", u=2, e=2),
-        )
-        for k in range(3):
+        for u in range(2):
+            nc.sync.dma_start(
+                out=wi_sb[:, u * 2 * FEAT : (u + 1) * 2 * FEAT].rearrange("p (e h) -> p e h", e=2),
+                in_=Wi[u * 2 * P : (u + 1) * 2 * P, :].rearrange("(p e) h -> p e h", e=2),
+            )
             load_next()
+        load_next()
         wo_sb = rows.tile([P, 4 * CHAN], BF16, tag="rows")
         nc.sync.dma_start(
             out=wo_sb[:].rearrange("p (a c) -> p a c", a=4),
@@ -307,8 +308,11 @@ def tile_slru_t_kernel(tc, inputs, Wi, bi, Wo, bo, params_log, out):
                     nc.vector.tensor_tensor(out=o_tiles[b][:, t, :], in0=o_ps[:], in1=bo32[:], op=ALU.add)
                 else:
                     nc.scalar.copy(out=o_tiles[b][:, t, :], in_=o_ps[:])
+                if b == n_blocks - 1:
+                    store(b, t, t + 1)
             for b in blocks:
-                store(b, 0, v_tiles(b))
+                if b < n_blocks - 1:
+                    store(b, 0, v_tiles(b))
 
         def gp_add(b):
             if G_TILES[b] > 0:

from contextlib import ExitStack

import concourse.mybir as mybir
from concourse.masks import make_identity

F32 = mybir.dt.float32
BF16 = mybir.dt.bfloat16
U32 = mybir.dt.uint32
U8 = mybir.dt.uint8
FP8X4 = mybir.dt.float8_e4m3fn_x4
ACT = mybir.ActivationFunctionType
ALU = mybir.AluOpType

P = 128
FEAT = 512
CHAN = 512
TOKENS = 8192
SEQ = 4096
HALF = 256
SIZES = (256, 256) + (512,) * 15
STARTS = tuple(sum(SIZES[:b]) for b in range(len(SIZES)))
GROUPS = ((0,), (1,), (2,), (3, 4), (5, 6), (7, 8), (9, 10), (11, 12), (13, 14), (15,), (16,))
G_TILES = (1, 1, 2) + (3, 3) * 4 + (2, 2) * 2 + (2, 0)
S_SHARE = (0, 0, 128, 512, 512, 512, 512, 512, 768, 512, 384)
ROW_BUFS = 12
FLOPS = 2 * TOKENS * FEAT * CHAN * 2


def tile_slru_t_kernel(tc, inputs, Wi, bi, Wo, bo, params_log, out):
    nc = tc.nc
    x_flat = inputs.flatten_outer_dims()
    out_flat = out.flatten_outer_dims()
    n_blocks = len(SIZES)
    n_groups = len(GROUPS)
    where = {}
    group_len = []
    for gi in range(n_groups):
        off = 0
        for b in GROUPS[gi]:
            where[b] = (gi, off)
            off += SIZES[b]
        group_len.append(off)

    def group(i):
        return GROUPS[i] if 0 <= i < n_groups else ()

    with ExitStack() as ctx:
        const = ctx.enter_context(tc.tile_pool(name="const", bufs=1))
        rows = ctx.enter_context(tc.tile_pool(name="rows", bufs=ROW_BUFS))
        grp = ctx.enter_context(tc.tile_pool(name="grp", bufs=2))
        xgp = ctx.enter_context(tc.tile_pool(name="xgp", bufs=3))
        mxin = ctx.enter_context(tc.tile_pool(name="mxin", bufs=3))
        upool = ctx.enter_context(tc.tile_pool(name="upool", bufs=2))
        xpool = ctx.enter_context(tc.tile_pool(name="xpool", bufs=3))
        opool = ctx.enter_context(tc.tile_pool(name="opool", bufs=4))
        ps_l = ctx.enter_context(tc.psum_pool(name="ps_l", bufs=1))
        ps = ctx.enter_context(tc.psum_pool(name="ps", bufs=7))
        ctx.enter_context(tc.manual_schedule())

        ident = const.tile([P, P], F32)
        make_identity(nc, ident[:])
        prow = const.tile([P, 2 * P], BF16)
        nc.vector.memset(prow[:], 0.0)
        lam_pad = const.tile([P, P], F32)
        nc.vector.memset(lam_pad[:], 0.0)
        bo_row = const.tile([P, FEAT], BF16)
        nc.vector.memset(bo_row[:], 0.0)
        ones = const.tile([P, P], BF16)
        nc.vector.memset(ones[:], 1.0)
        nc.scalar.dma_start(out=prow[0:4, :], in_=params_log.rearrange("v (u w) -> (v u) w", u=2))
        nc.scalar.dma_start(out=prow[4:6, :], in_=bi.rearrange("(u w) -> u w", u=2))
        nc.scalar.dma_start(out=bo_row[0:1, :], in_=bo.rearrange("(o f) -> o f", o=1))

        x_sb = {}
        loaded = [0]

        def load_next():
            b = loaded[0]
            if b >= n_blocks:
                return
            loaded[0] = b + 1
            pieces = SIZES[b] // P
            x_tile = rows.tile([P, pieces * FEAT], BF16, tag="rows")
            nc.sync.dma_start(
                out=x_tile[:].rearrange("p (s h) -> p s h", s=pieces),
                in_=x_flat[STARTS[b] : STARTS[b] + SIZES[b], :].rearrange("(s p) h -> p s h", p=P),
            )
            x_sb[b] = x_tile

        wi_sb = rows.tile([P, 4 * FEAT], BF16, tag="rows")
        for u in range(2):
            nc.sync.dma_start(
                out=wi_sb[:, u * 2 * FEAT : (u + 1) * 2 * FEAT].rearrange("p (e h) -> p e h", e=2),
                in_=Wi[u * 2 * P : (u + 1) * 2 * P, :].rearrange("(p e) h -> p e h", e=2),
            )
            load_next()
        load_next()
        wo_sb = rows.tile([P, 4 * CHAN], BF16, tag="rows")
        nc.sync.dma_start(
            out=wo_sb[:].rearrange("p (a c) -> p a c", a=4),
            in_=Wo.rearrange("(a p) c -> p a c", p=P),
        )
        for k in range(ROW_BUFS - 5):
            load_next()

        warm = const.tile([P, 1], F32)
        nc.scalar.activation(out=warm[:], in_=lam_pad[:, 0:1], func=ACT.Exp)

        def transpose_half(src, half):
            bank = ps.tile([P, 2, 2, P], F32, tag="bank")
            src32 = src[:].bitcast(F32)
            for s2 in range(2):
                for u in range(2):
                    first = (2 * half + s2) * 256 + u * P
                    nc.tensor.transpose(bank[:, s2, u, :], src32[:, first : first + P], ident[:])
            return bank

        def copy_half(on_scalar, g_tile, half, bank):
            g32 = g_tile[:].bitcast(F32).rearrange("p (c u) -> p c u", u=2)
            dst = g32[:, half * HALF : (half + 1) * HALF, :].rearrange("p (s r) u -> p s r u", s=2)
            view = bank[:].rearrange("p s u r -> p s r u")
            if on_scalar:
                nc.scalar.copy(out=dst, in_=view)
            else:
                nc.vector.tensor_copy(out=dst, in_=view)

        def quantise(src, codes, scales):
            nc.vector.quantize_mx(out=codes.bitcast(FP8X4), scales=scales, in_=src)

        grouped = {}
        in_mx = {}

        def new_grouped(b):
            g_tile = grp.tile([P, 4 * SIZES[b]], BF16, align_bytes=64, tag="grouped")
            grouped[b] = g_tile

        def q1(b):
            in_codes = mxin.tile([P, SIZES[b]], U32, align_bytes=64, tag="in_codes")
            in_scales = mxin.tile([P, SIZES[b]], U8, align_bytes=64, tag="in_scales")
            quantise(grouped[b][:], in_codes[:], in_scales[:])
            in_mx[b] = (in_codes, in_scales)

        wi_codes = const.tile([P, CHAN], U32, align_bytes=64)
        wi_scales = const.tile([P, CHAN], U8, align_bytes=64)
        wo_codes = const.tile([P, FEAT], U32, align_bytes=64)
        wo_scales = const.tile([P, FEAT], U8, align_bytes=64)

        def quantise_weight_half(g_tile, codes, scales, h):
            quantise(
                g_tile[:, h * 4 * HALF : (h + 1) * 4 * HALF],
                codes[:, h * HALF : (h + 1) * HALF],
                scales[:, h * HALF : (h + 1) * HALF],
            )

        wi_g = grp.tile([P, 4 * CHAN], BF16, align_bytes=64, tag="grouped")
        bank = transpose_half(wi_sb, 0)
        copy_half(True, wi_g, 0, bank)
        new_grouped(0)
        bank = transpose_half(x_sb[0], 0)
        copy_half(False, grouped[0], 0, bank)
        load_next()
        pbank = ps.tile([P, FEAT], F32, tag="bank")
        nc.tensor.transpose(pbank[:, 0:P], prow[:].bitcast(F32), ident[:])
        pwords = const.tile([P, 8], F32)
        nc.vector.tensor_copy(out=pwords[:], in_=pbank[:, 0:8])
        pcol = pwords[:].bitcast(BF16)
        nu = const.tile([P, 4], F32)
        nc.scalar.activation(out=nu[:], in_=pcol[:, 0:4], func=ACT.Exp)
        nc.scalar.activation(out=lam_pad[:, 0:4], in_=nu[:], func=ACT.Exp, scale=-1.0)
        gam = const.tile([P, 4], F32)
        nc.scalar.activation(out=gam[:], in_=pcol[:, 4:8], func=ACT.Exp)
        bank = transpose_half(wi_sb, 1)
        copy_half(True, wi_g, 1, bank)
        load_next()
        quantise_weight_half(wi_g, wi_codes, wi_scales, 0)
        q1(0)
        gbi = const.tile([P, 4], F32)
        nc.vector.tensor_tensor(out=gbi[:], in0=gam[:], in1=pcol[:, 8:12], op=ALU.mult)
        lbank = ps.tile([P, FEAT], F32, tag="bank")
        nc.tensor.transpose(lbank[:, 0:P], lam_pad[:], ident[:])
        lam_rows = const.tile([P, P], F32)
        nc.vector.tensor_copy(out=lam_rows[:], in_=lbank[:, 0:P])
        lam_ps = ps_l.tile([P, P], F32)
        nc.tensor.transpose(lam_ps[:], lam_rows[:], ident[:])
        quantise_weight_half(wi_g, wi_codes, wi_scales, 1)
        new_grouped(1)
        bank = transpose_half(x_sb[1], 0)
        copy_half(False, grouped[1], 0, bank)
        load_next()
        q1(1)

        bo32 = const.tile([P, FEAT], F32)
        u_tiles = {}
        xs_tiles = {}
        xg = {}
        x_mx = {}
        o_tiles = {}

        def phase1(c_blocks, a_blocks):
            for b2 in a_blocks:
                new_grouped(b2)
                for h in range(SIZES[b2] // HALF):
                    bank_a = transpose_half(x_sb[b2], h)
                    copy_half(True, grouped[b2], h, bank_a)
                load_next()
            for b in c_blocks:
                gi, off = where[b]
                if gi not in u_tiles:
                    u_sb = upool.tile([P, 4, group_len[gi]], F32, tag="u_sb")
                    u_tiles[gi] = u_sb
                for j in range(4):
                    u_ps = ps.tile([P, SIZES[b]], F32, tag="bank")
                    nc.tensor.matmul_mx(
                        out=u_ps[:],
                        lhsT=wi_codes[:, j * P : (j + 1) * P].bitcast(FP8X4),
                        lhsT_scale=wi_scales[:, j * P : (j + 1) * P],
                        rhs=in_mx[b][0][:].bitcast(FP8X4),
                        rhs_scale=in_mx[b][1][:],
                        start=True,
                        stop=True,
                    )
                    nc.scalar.activation(
                        out=u_tiles[gi][:, j, off : off + SIZES[b]],
                        in_=u_ps[:],
                        func=ACT.Identity,
                        bias=gbi[:, j : j + 1],
                        scale=gam[:, j : j + 1],
                    )

        def scan(gi):
            n = group_len[gi]
            xs = xpool.tile([P, 4, n], F32, tag="xs")
            xs_tiles[gi] = xs
            first = STARTS[GROUPS[gi][0]] % SEQ == 0
            for j in range(4):
                if first:
                    start_value = 0.0
                else:
                    n_prev = group_len[gi - 1]
                    start_value = xs_tiles[gi - 1][:, j, n_prev - 1 : n_prev]
                nc.vector.tensor_tensor_scan(
                    out=xs[:, j, :],
                    data0=lam_ps[:, j : j + 1].to_broadcast([P, n]),
                    data1=u_tiles[gi][:, j, :],
                    initial=start_value,
                    op0=ALU.mult,
                    op1=ALU.add,
                )

        def regroup_scalar(gi):
            n = group_len[gi]
            lo = n - S_SHARE[gi]
            if lo < n:
                nc.scalar.copy(
                    out=xg[gi][:, lo:n, :].rearrange("p (c i) j -> p c j i", i=4),
                    in_=xs_tiles[gi][:, :, lo:n].rearrange("p j (c i) -> p c j i", i=4),
                )

        def regroup_gpsimd(gi):
            n_g = group_len[gi] - S_SHARE[gi]
            if n_g > 0:
                nc.gpsimd.tensor_scalar(
                    out=xg[gi][:, 0:n_g, :],
                    in0=xs_tiles[gi][:, :, 0:n_g].rearrange("p j t -> p t j"),
                    scalar1=1.0,
                    scalar2=0.0,
                    op0=ALU.mult,
                    op1=ALU.add,
                )

        def q2(b):
            x_codes = mxin.tile([P, SIZES[b]], U32, align_bytes=64, tag="x_codes")
            x_scales = mxin.tile([P, SIZES[b]], U8, align_bytes=64, tag="x_scales")
            gi, off = where[b]
            quantise(xg[gi][:, off : off + SIZES[b], :].rearrange("p t j -> p (t j)"), x_codes[:], x_scales[:])
            x_mx[b] = (x_codes, x_scales)

        def store(b, t0, t1):
            nc.sync.dma_start(
                out=out_flat[STARTS[b] + t0 * P : STARTS[b] + t1 * P, :].rearrange("(s p) f -> p s f", p=P),
                in_=o_tiles[b][:, t0:t1, :],
            )

        def v_tiles(b):
            return SIZES[b] // P - G_TILES[b]

        def stage2(blocks):
            order = []
            for b in blocks:
                order.extend([(b, t) for t in range(v_tiles(b))])
            for b in blocks:
                order.extend([(b, t) for t in range(v_tiles(b), SIZES[b] // P)])
            for b in blocks:
                o_sb = opool.tile([P, SIZES[b] // P, FEAT], F32, tag="o_sb")
                o_tiles[b] = o_sb
            for b, t in order:
                o_ps = ps.tile([P, FEAT], F32, tag="bank")
                nc.tensor.matmul_mx(
                    out=o_ps[:],
                    lhsT=x_mx[b][0][:, t * P : (t + 1) * P].bitcast(FP8X4),
                    lhsT_scale=x_mx[b][1][:, t * P : (t + 1) * P],
                    rhs=wo_codes[:].bitcast(FP8X4),
                    rhs_scale=wo_scales[:],
                    start=True,
                    stop=True,
                )
                if t < v_tiles(b):
                    nc.vector.tensor_tensor(out=o_tiles[b][:, t, :], in0=o_ps[:], in1=bo32[:], op=ALU.add)
                else:
                    nc.scalar.copy(out=o_tiles[b][:, t, :], in_=o_ps[:])
                if b == n_blocks - 1:
                    store(b, t, t + 1)
            for b in blocks:
                if b < n_blocks - 1:
                    store(b, 0, v_tiles(b))

        def gp_add(b):
            if G_TILES[b] > 0:
                part = o_tiles[b][:, v_tiles(b) : SIZES[b] // P, :]
                nc.gpsimd.tensor_tensor(
                    out=part, in0=part, in1=bo32[:].unsqueeze(1).to_broadcast([P, G_TILES[b], FEAT]), op=ALU.add
                )
                store(b, v_tiles(b), SIZES[b] // P)

        for s in range(-1, n_groups + 2):
            a_blocks = group(s + 2) if s >= 0 else ()
            phase1(group(s + 1), a_blocks)
            if s == 0:
                wo_g = xgp.tile([P, 4 * FEAT], BF16, align_bytes=64, tag="xg")
                for h in range(2):
                    bank = transpose_half(wo_sb, h)
                    copy_half(True, wo_g, h, bank)
                load_next()
                bo_ps = ps.tile([P, FEAT], F32, tag="bank")
                nc.tensor.matmul(out=bo_ps[:], lhsT=ones[:], rhs=bo_row[:], start=True, stop=True)
                nc.scalar.copy(out=bo32[:], in_=bo_ps[:])
            if 0 <= s < n_groups:
                scan(s)
                xg_tile = xgp.tile([P, group_len[s], 4], BF16, align_bytes=64, tag="xg")
                xg[s] = xg_tile
                regroup_scalar(s)
            if 0 <= s - 1 < n_groups:
                regroup_gpsimd(s - 1)
            for b in group(s - 2):
                gp_add(b)
            done = group(s - 1)
            if s == 1:
                quantise(wo_g[:], wo_codes[:], wo_scales[:])
            for b in done:
                q2(b)
            for b in a_blocks:
                q1(b)
            if 0 <= s < n_groups and S_SHARE[s] < group_len[s]:
                nc.vector.memset(xg[s][:].rearrange("p t j -> p (t j)")[:, 0:2].bitcast(F32), 0.0)
            if len(done) > 0:
                stage2(done)
